import numpy as np
import ml_dtypes


def mxq(x, axis, fmt="e4m3"):
    dtype, down = {"e4m3": (ml_dtypes.float8_e4m3fn, 7), "e5m2": (ml_dtypes.float8_e5m2, 14)}[fmt]
    v = np.moveaxis(np.asarray(x, np.float32).astype(ml_dtypes.bfloat16).astype(np.float64), axis, -1)
    blocks = v.reshape(v.shape[:-1] + (-1, 32))
    amax = np.abs(blocks).max(-1, keepdims=True)
    byte = np.maximum(np.where(amax > 0, np.frexp(amax)[1] - 1 + 127, 0) - down, 1)
    scale = np.exp2(byte - 127.0)
    codes = (blocks / scale).astype(np.float32).astype(dtype).astype(np.float64)
    return np.moveaxis((codes * scale).reshape(v.shape), -1, axis)


WIDE = False


def mx_kscale(k):
    if not WIDE:
        return np.ones(k)
    levels = np.array([10, -10, 5, -5, 0])
    a = np.random.permutation(np.resize(levels, k // 512 * 4)).reshape(k // 512, 4)
    idx = np.arange(k)
    return np.exp2(a[idx // 512, idx % 128 // 32])


BF16 = ml_dtypes.bfloat16


def bf(x):
    return np.asarray(x, np.float32).astype(BF16)


def f64(x):
    return np.asarray(x).astype(np.float64)


B, T, HP, WP, NH, G, HD = 2, 2, 8, 16, 16, 4, 32
D = NH * HD
S = HP * WP
AX = HD // 3
E = (NH + 2 * G) * HD
ROPE_THETA = 10000.0
QK_NORM_EPS = 1e-10


def qk_norm(v):
    n = np.sqrt(np.sum(v * v, axis=-1, keepdims=True))
    return v / np.maximum(n, QK_NORM_EPS)


def rope_spatial(v):
    nf, ns, nh, hd = v.shape
    vs = v.reshape(nf, HP, WP, nh, hd).transpose(0, 3, 1, 2, 4)
    inv_freq = 1.0 / (ROPE_THETA ** (np.arange(0, AX, 2, dtype=np.float64) / AX))
    freqs_h = np.arange(HP, dtype=np.float64)[:, None] * inv_freq[None, :]
    freqs_w = np.arange(WP, dtype=np.float64)[:, None] * inv_freq[None, :]
    freqs = freqs_h[:, None, :] + freqs_w[None, :, :]
    cos = np.cos(freqs)[None, None]
    sin = np.sin(freqs)[None, None]
    v_axis = vs[..., :AX]
    v1 = v_axis[..., 0::2]
    v2 = v_axis[..., 1::2]
    rot = np.concatenate([v1 * cos - v2 * sin, v1 * sin + v2 * cos], axis=-1)
    res = np.concatenate([rot, vs[..., AX:]], axis=-1)
    return res.transpose(0, 2, 3, 1, 4).reshape(nf, ns, nh, hd)


def setup_inputs():
    s = mx_kscale(D)
    return {"x": bf(np.random.standard_normal((B, T, S, D)) * s),
            "w_qkv": bf(np.random.standard_normal((E, D)) / np.sqrt(D) / s[None, :])}


def reference(x, w_qkv):
    nf = B * T
    xf = f64(x).reshape(nf, S, D)
    qkv = mxq(xf, 2, "e4m3") @ mxq(f64(w_qkv), 1, "e4m3").T
    q_dim = NH * HD
    g_dim = G * HD
    q = qkv[..., :q_dim].reshape(nf, S, NH, HD)
    k = qkv[..., q_dim:q_dim + g_dim].reshape(nf, S, G, HD)
    v = qkv[..., q_dim + g_dim:].reshape(nf, S, G, HD)
    q_rot = rope_spatial(qk_norm(q))
    k_rot = rope_spatial(qk_norm(k))
    return q_rot, k_rot, v

@@ -1,0 +1,206 @@
+import math
+
+import concourse.mybir as mybir
+from concourse.masks import make_identity
+
+F32 = mybir.dt.float32
+BF16 = mybir.dt.bfloat16
+I32 = mybir.dt.int32
+U32 = mybir.dt.uint32
+U8 = mybir.dt.uint8
+FP8X4 = mybir.dt.float8_e4m3fn_x4
+ALU = mybir.AluOpType
+FUNC = mybir.ActivationFunctionType
+AXIS = mybir.AxisListType
+
+P = 128
+FRAMES = 4
+D = 512
+HALVES = 2
+HD = 32
+HEADS = 16
+GRID_W = 16
+FREQS = 5
+ROT = 2 * FREQS
+W_TILES = 6
+ROPE_THETA = 10000.0
+QK_NORM_EPS = 1e-10
+ROUND_MAGIC = 12582912.0
+
+FLOPS = 2 * FRAMES * P * D * W_TILES * P
+
+
+def tile_spatiotemporalattention_pa_s_kernel(tc, x, w_qkv, out_0, out_1, out_2):
+    nc = tc.nc
+    x_tiles = x.rearrange("b t s d -> s (b t) d")
+    w_tiles = w_qkv.rearrange("(t r) d -> r t d", r=P)
+
+    with tc.tile_pool(name="keep", bufs=1) as keep, tc.tile_pool(
+        name="unit", bufs=FRAMES + 1
+    ) as unit, tc.psum_pool(name="flip", bufs=2) as flip, tc.psum_pool(name="acc", bufs=1) as acc:
+        x_sb = keep.tile([P, FRAMES, D], BF16)
+        w_sb = keep.tile([P, W_TILES, D], BF16)
+        nc.sync.dma_start(out=x_sb[:, 0:1, :], in_=x_tiles[:, 0:1, :])
+        nc.sync.dma_start(out=w_sb[:, 0:2, :], in_=w_tiles[:, 0:2, :])
+        nc.sync.dma_start(out=w_sb[:, 2:4, :], in_=w_tiles[:, 2:4, :])
+        nc.sync.dma_start(out=x_sb[:, 1:2, :], in_=x_tiles[:, 1:2, :])
+        nc.sync.dma_start(out=x_sb[:, 2:4, :], in_=x_tiles[:, 2:4, :])
+        nc.sync.dma_start(out=w_sb[:, 4:6, :], in_=w_tiles[:, 4:6, :])
+
+        zero = keep.tile([P, 1], F32)
+        nc.vector.memset(zero[:], 0.0)
+        warm_sin = keep.tile([P, 1], F32)
+        nc.scalar.activation(out=warm_sin[:], in_=zero[:], func=FUNC.Sin)
+
+        patch = keep.tile([P, 1], I32)
+        nc.gpsimd.iota(patch[:], pattern=[[0, 1]], base=0, channel_multiplier=1)
+        ident = keep.tile([P, P], F32)
+        make_identity(nc, ident[:])
+
+        grid_row = keep.tile([P, 1], I32)
+        nc.vector.tensor_single_scalar(
+            out=grid_row[:], in_=patch[:], scalar=4, op=ALU.arith_shift_right
+        )
+        steps = keep.tile([P, 1], F32)
+        nc.vector.scalar_tensor_tensor(
+            out=steps[:],
+            in0=grid_row[:],
+            scalar=float(1 - GRID_W),
+            in1=patch[:],
+            op0=ALU.mult,
+            op1=ALU.add,
+        )
+        quarter = keep.tile([P, 2], F32)
+        nc.vector.memset(quarter[:, 0:1], 0.25)
+        nc.vector.memset(quarter[:, 1:2], 0.0)
+        turns = keep.tile([P, 2, FREQS], F32)
+        for m in range(FREQS):
+            nc.vector.scalar_tensor_tensor(
+                out=turns[:, :, m],
+                in0=steps[:, 0:1].to_broadcast([P, 2]),
+                scalar=ROPE_THETA ** (-2.0 * m / ROT) / (2.0 * math.pi),
+                in1=quarter[:],
+                op0=ALU.mult,
+                op1=ALU.add,
+            )
+        whole = keep.tile([P, 2, FREQS], F32)
+        nc.vector.tensor_scalar(
+            out=whole[:],
+            in0=turns[:],
+            scalar1=ROUND_MAGIC,
+            scalar2=ROUND_MAGIC,
+            op0=ALU.add,
+            op1=ALU.subtract,
+        )
+        part = keep.tile([P, 2, FREQS], F32)
+        nc.vector.tensor_tensor(out=part[:], in0=turns[:], in1=whole[:], op=ALU.subtract)
+        table = keep.tile([P, 3, FREQS], F32)
+        nc.scalar.activation(out=table[:, 1:3, :], in_=part[:], func=FUNC.Sin, scale=2.0 * math.pi)
+        nc.scalar.activation(
+            out=table[:, 0, :], in_=part[:, 1, :], func=FUNC.Sin, scale=-2.0 * math.pi
+        )
+        warm_sqrt = keep.tile([P, 1], F32)
+        nc.scalar.activation(
+            out=warm_sqrt[:], in_=table[:, 0, 0:1], func=FUNC.Sqrt, scale=0.0, bias=1.0
+        )
+        cos_sin = table[:, 1:3, :].unsqueeze(1).to_broadcast([P, HEADS, 2, FREQS])
+        nsin_cos = table[:, 0:2, :].unsqueeze(1).to_broadcast([P, HEADS, 2, FREQS])
+
+        x_grouped = keep.tile([P, FRAMES * D], BF16, align_bytes=64)
+        w_grouped = keep.tile([P, W_TILES * D], BF16, align_bytes=64)
+        x_codes = keep.tile([P, FRAMES * P], U32, align_bytes=64)
+        w_codes = keep.tile([P, W_TILES * P], U32, align_bytes=64)
+        x_scales = keep.tile([P, FRAMES * P], U8, align_bytes=64)
+        w_scales = keep.tile([P, W_TILES * P], U8, align_bytes=64)
+
+        def quantise_tiles(rows_sb, first, count, grouped, codes, scales, copy):
+            flipped = flip.tile([P, 2, HALVES, P], F32)
+            for i in range(count):
+                words = rows_sb[:, first + i, :].bitcast(F32)
+                for u in range(HALVES):
+                    nc.tensor.transpose(flipped[:, i, u, :], words[:, u * P : (u + 1) * P], ident[:])
+            copy(
+                out=grouped[:, first * D : (first + count) * D]
+                .bitcast(F32)
+                .rearrange("p (i r u) -> p i r u", r=P, u=HALVES),
+                in_=flipped[:, 0:count].rearrange("p i u r -> p i r u"),
+            )
+            nc.vector.quantize_mx(
+                out=codes[:, first * P : (first + count) * P].bitcast(FP8X4),
+                scales=scales[:, first * P : (first + count) * P],
+                in_=grouped[:, first * D : (first + count) * D],
+            )
+
+        def project(out, frame, first_col, cols):
+            nc.tensor.matmul_mx(
+                out=out,
+                lhsT=x_codes[:, frame * P : (frame + 1) * P].bitcast(FP8X4),
+                lhsT_scale=x_scales[:, frame * P : (frame + 1) * P],
+                rhs=w_codes[:, first_col : first_col + cols].bitcast(FP8X4),
+                rhs_scale=w_scales[:, first_col : first_col + cols],
+                start=True,
+                stop=True,
+            )
+
+        def norm_and_rope(raw):
+            squares = unit.tile([P, HEADS, HD], F32)
+            nc.scalar.activation(
+                out=squares[:], in_=raw.rearrange("p (h c) -> p h c", c=HD), func=FUNC.Square
+            )
+            sumsq = unit.tile([P, HEADS], F32)
+            nc.vector.tensor_reduce(out=sumsq[:], in_=squares[:], axis=AXIS.X, op=ALU.add)
+            norm = unit.tile([P, HEADS], F32)
+            nc.scalar.activation(out=norm[:], in_=sumsq[:], func=FUNC.Sqrt)
+            inv = unit.tile([P, HEADS], F32)
+            nc.vector.reciprocal(out=inv[:], in_=norm[:])
+            res = unit.tile([P, HEADS, HD], F32)
+            nc.vector.scalar_tensor_tensor(
+                out=res[:],
+                in0=inv[:].unsqueeze(2).to_broadcast([P, HEADS, HD]),
+                scalar=1.0 / QK_NORM_EPS,
+                in1=raw.rearrange("p (h c) -> p h c", c=HD),
+                op0=ALU.min,
+                op1=ALU.mult,
+            )
+            pairs = res[:, :, 0:ROT].rearrange("p h (m e) -> p h m e", e=2)
+            even = pairs[:, :, :, 0].unsqueeze(2).to_broadcast([P, HEADS, 2, FREQS])
+            odd = pairs[:, :, :, 1].unsqueeze(2).to_broadcast([P, HEADS, 2, FREQS])
+            from_even = unit.tile([P, HEADS, 2, FREQS], F32)
+            from_odd = unit.tile([P, HEADS, 2, FREQS], F32)
+            nc.vector.tensor_tensor(out=from_even[:], in0=even, in1=cos_sin, op=ALU.mult)
+            nc.vector.tensor_tensor(out=from_odd[:], in0=odd, in1=nsin_cos, op=ALU.mult)
+            nc.vector.tensor_tensor(
+                out=res[:, :, 0:ROT].rearrange("p h (o m) -> p h o m", o=2),
+                in0=from_even[:],
+                in1=from_odd[:],
+                op=ALU.add,
+            )
+            return res
+
+        quantise_tiles(x_sb, 0, 1, x_grouped, x_codes, x_scales, nc.vector.tensor_copy)
+        quantise_tiles(w_sb, 0, 2, w_grouped, w_codes, w_scales, nc.scalar.copy)
+        quantise_tiles(w_sb, 2, 2, w_grouped, w_codes, w_scales, nc.scalar.copy)
+        quantise_tiles(x_sb, 1, 1, x_grouped, x_codes, x_scales, nc.scalar.copy)
+        quantise_tiles(x_sb, 2, 2, x_grouped, x_codes, x_scales, nc.scalar.copy)
+        quantise_tiles(w_sb, 4, 2, w_grouped, w_codes, w_scales, nc.scalar.copy)
+
+        for f in range(FRAMES):
+            q_raw = acc.tile([P, HEADS * HD], F32, name="q_raw%d" % f)
+            project(q_raw[:], f, 0, HEADS * HD)
+            q_res = norm_and_rope(q_raw[:])
+            nc.sync.dma_start(out=out_0[f].rearrange("s h c -> s (h c)"), in_=q_res[:].rearrange("p h c -> p (h c)"))
+
+        k_raw = acc.tile([P, FRAMES * P], F32)
+        v_raw = acc.tile([P, FRAMES * P], F32)
+        for f in range(FRAMES):
+            project(k_raw[:, f * P : (f + 1) * P], f, 4 * P, P)
+        for f in range(FRAMES):
+            project(v_raw[:, f * P : (f + 1) * P], f, 5 * P, P)
+        v_res = keep.tile([P, FRAMES, P], F32)
+        nc.scalar.copy(out=v_res[:], in_=v_raw[:].rearrange("p (f c) -> p f c", c=P))
+        nc.sync.dma_start(out=out_2.rearrange("f s g c -> s f (g c)"), in_=v_res[:])
+        k_res = norm_and_rope(k_raw[:])
+        nc.sync.dma_start(
+            out=out_1.rearrange("f s g c -> s f (g c)"),
+            in_=k_res[:].rearrange("p (f g) c -> p f (g c)", f=FRAMES),
+        )

@@ -22,6 +22,9 @@ HEADS = 16
 GRID_W = 16
 FREQS = 5
 ROT = 2 * FREQS
+UNITS = FRAMES + 1
+BANKS = 8
+POOL_UNITS = 4
 W_TILES = 6
 ROPE_THETA = 10000.0
 QK_NORM_EPS = 1e-10
@@ -36,14 +39,14 @@ def tile_spatiotemporalattention_pa_s_kernel(tc, x, w_qkv, out_0, out_1, out_2):
     w_tiles = w_qkv.rearrange("(t r) d -> r t d", r=P)
 
     with tc.tile_pool(name="keep", bufs=1) as keep, tc.tile_pool(
-        name="unit", bufs=FRAMES + 1
-    ) as unit, tc.psum_pool(name="flip", bufs=2) as flip, tc.psum_pool(name="acc", bufs=1) as acc:
+        name="unit", bufs=UNITS
+    ) as unit, tc.psum_pool(name="psum", bufs=BANKS) as psum, tc.manual_schedule():
         x_sb = keep.tile([P, FRAMES, D], BF16)
         w_sb = keep.tile([P, W_TILES, D], BF16)
-        nc.sync.dma_start(out=x_sb[:, 0:1, :], in_=x_tiles[:, 0:1, :])
-        nc.sync.dma_start(out=w_sb[:, 0:2, :], in_=w_tiles[:, 0:2, :])
-        nc.sync.dma_start(out=w_sb[:, 2:4, :], in_=w_tiles[:, 2:4, :])
-        nc.sync.dma_start(out=x_sb[:, 1:2, :], in_=x_tiles[:, 1:2, :])
+        nc.sync.dma_start(out=x_sb[:, 0, :], in_=x_tiles[:, 0, :])
+        for t in range(4):
+            nc.sync.dma_start(out=w_sb[:, t, :], in_=w_tiles[:, t, :])
+        nc.sync.dma_start(out=x_sb[:, 1, :], in_=x_tiles[:, 1, :])
         nc.sync.dma_start(out=x_sb[:, 2:4, :], in_=x_tiles[:, 2:4, :])
         nc.sync.dma_start(out=w_sb[:, 4:6, :], in_=w_tiles[:, 4:6, :])
 
@@ -99,10 +102,10 @@ def tile_spatiotemporalattention_pa_s_kernel(tc, x, w_qkv, out_0, out_1, out_2):
         nc.scalar.activation(
             out=table[:, 0, :], in_=part[:, 1, :], func=FUNC.Sin, scale=-2.0 * math.pi
         )
-        warm_sqrt = keep.tile([P, 1], F32)
-        nc.scalar.activation(
-            out=warm_sqrt[:], in_=table[:, 0, 0:1], func=FUNC.Sqrt, scale=0.0, bias=1.0
-        )
+        one = keep.tile([P, 1], F32)
+        nc.vector.memset(one[:], 1.0)
+        warm_rsqrt = keep.tile([P, 1], F32)
+        nc.scalar.activation(out=warm_rsqrt[:], in_=one[:], func=FUNC.Abs_reciprocal_sqrt)
         cos_sin = table[:, 1:3, :].unsqueeze(1).to_broadcast([P, HEADS, 2, FREQS])
         nsin_cos = table[:, 0:2, :].unsqueeze(1).to_broadcast([P, HEADS, 2, FREQS])
 
@@ -113,23 +116,28 @@ def tile_spatiotemporalattention_pa_s_kernel(tc, x, w_qkv, out_0, out_1, out_2):
         x_scales = keep.tile([P, FRAMES * P], U8, align_bytes=64)
         w_scales = keep.tile([P, W_TILES * P], U8, align_bytes=64)
 
-        def quantise_tiles(rows_sb, first, count, grouped, codes, scales, copy):
-            flipped = flip.tile([P, 2, HALVES, P], F32)
-            for i in range(count):
-                words = rows_sb[:, first + i, :].bitcast(F32)
-                for u in range(HALVES):
-                    nc.tensor.transpose(flipped[:, i, u, :], words[:, u * P : (u + 1) * P], ident[:])
+        def quantise_tile(rows_sb, t, grouped, codes, scales, copy):
+            words = rows_sb[:, t, :].bitcast(F32)
+            flipped = psum.tile([P, HALVES, P], F32, tag="bank")
+            for u in range(HALVES):
+                nc.tensor.transpose(flipped[:, u, :], words[:, u * P : (u + 1) * P], ident[:])
             copy(
-                out=grouped[:, first * D : (first + count) * D]
+                out=grouped[:, t * D : (t + 1) * D]
                 .bitcast(F32)
-                .rearrange("p (i r u) -> p i r u", r=P, u=HALVES),
-                in_=flipped[:, 0:count].rearrange("p i u r -> p i r u"),
+                .rearrange("p (r u) -> p r u", u=HALVES),
+                in_=flipped[:].rearrange("p u r -> p r u"),
             )
             nc.vector.quantize_mx(
-                out=codes[:, first * P : (first + count) * P].bitcast(FP8X4),
-                scales=scales[:, first * P : (first + count) * P],
-                in_=grouped[:, first * D : (first + count) * D],
+                out=codes[:, t * P : (t + 1) * P].bitcast(FP8X4),
+                scales=scales[:, t * P : (t + 1) * P],
+                in_=grouped[:, t * D : (t + 1) * D],
             )
+
+        def quantise_x(f, copy):
+            quantise_tile(x_sb, f, x_grouped, x_codes, x_scales, copy)
+
+        def quantise_w(t, copy):
+            quantise_tile(w_sb, t, w_grouped, w_codes, w_scales, copy)
 
         def project(out, frame, first_col, cols):
             nc.tensor.matmul_mx(
@@ -142,65 +150,90 @@ def tile_spatiotemporalattention_pa_s_kernel(tc, x, w_qkv, out_0, out_1, out_2):
                 stop=True,
             )
 
-        def norm_and_rope(raw):
+        raws = []
+        sumsqs = []
+        results = []
+
+        def project_queries(f):
+            q_raw = psum.tile([P, HEADS, HD], F32, tag="bank")
+            project(q_raw[:].rearrange("p h c -> p (h c)"), f, 0, HEADS * HD)
+            raws.append(q_raw)
+
+        def square_and_sum(u):
             squares = unit.tile([P, HEADS, HD], F32)
-            nc.scalar.activation(
-                out=squares[:], in_=raw.rearrange("p (h c) -> p h c", c=HD), func=FUNC.Square
-            )
+            nc.scalar.activation(out=squares[:], in_=raws[u][:], func=FUNC.Square)
             sumsq = unit.tile([P, HEADS], F32)
             nc.vector.tensor_reduce(out=sumsq[:], in_=squares[:], axis=AXIS.X, op=ALU.add)
-            norm = unit.tile([P, HEADS], F32)
-            nc.scalar.activation(out=norm[:], in_=sumsq[:], func=FUNC.Sqrt)
+            sumsqs.append(sumsq)
+
+        def normalise(u):
             inv = unit.tile([P, HEADS], F32)
-            nc.vector.reciprocal(out=inv[:], in_=norm[:])
+            nc.scalar.activation(out=inv[:], in_=sumsqs[u][:], func=FUNC.Abs_reciprocal_sqrt)
             res = unit.tile([P, HEADS, HD], F32)
             nc.vector.scalar_tensor_tensor(
                 out=res[:],
                 in0=inv[:].unsqueeze(2).to_broadcast([P, HEADS, HD]),
                 scalar=1.0 / QK_NORM_EPS,
-                in1=raw.rearrange("p (h c) -> p h c", c=HD),
+                in1=raws[u][:],
                 op0=ALU.min,
                 op1=ALU.mult,
             )
+            results.append(res)
+
+        def rotate_and_store(u):
+            engine = nc.gpsimd if u < POOL_UNITS else nc.vector
+            res = results[u]
             pairs = res[:, :, 0:ROT].rearrange("p h (m e) -> p h m e", e=2)
             even = pairs[:, :, :, 0].unsqueeze(2).to_broadcast([P, HEADS, 2, FREQS])
             odd = pairs[:, :, :, 1].unsqueeze(2).to_broadcast([P, HEADS, 2, FREQS])
             from_even = unit.tile([P, HEADS, 2, FREQS], F32)
             from_odd = unit.tile([P, HEADS, 2, FREQS], F32)
-            nc.vector.tensor_tensor(out=from_even[:], in0=even, in1=cos_sin, op=ALU.mult)
-            nc.vector.tensor_tensor(out=from_odd[:], in0=odd, in1=nsin_cos, op=ALU.mult)
-            nc.vector.tensor_tensor(
+            engine.tensor_tensor(out=from_even[:], in0=even, in1=cos_sin, op=ALU.mult)
+            engine.tensor_tensor(out=from_odd[:], in0=odd, in1=nsin_cos, op=ALU.mult)
+            engine.tensor_tensor(
                 out=res[:, :, 0:ROT].rearrange("p h (o m) -> p h o m", o=2),
                 in0=from_even[:],
                 in1=from_odd[:],
                 op=ALU.add,
             )
-            return res
+            if u < FRAMES:
+                nc.sync.dma_start(out=out_0[u], in_=res[:])
+            else:
+                nc.sync.dma_start(
+                    out=out_1.rearrange("f s g c -> s f (g c)"),
+                    in_=res[:].rearrange("p (f g) c -> p f (g c)", f=FRAMES),
+                )
 
-        quantise_tiles(x_sb, 0, 1, x_grouped, x_codes, x_scales, nc.vector.tensor_copy)
-        quantise_tiles(w_sb, 0, 2, w_grouped, w_codes, w_scales, nc.scalar.copy)
-        quantise_tiles(w_sb, 2, 2, w_grouped, w_codes, w_scales, nc.scalar.copy)
-        quantise_tiles(x_sb, 1, 1, x_grouped, x_codes, x_scales, nc.scalar.copy)
-        quantise_tiles(x_sb, 2, 2, x_grouped, x_codes, x_scales, nc.scalar.copy)
-        quantise_tiles(w_sb, 4, 2, w_grouped, w_codes, w_scales, nc.scalar.copy)
-
+        quantise_x(0, nc.vector.tensor_copy)
+        quantise_w(0, nc.vector.tensor_copy)
+        quantise_w(1, nc.scalar.copy)
+        quantise_w(2, nc.vector.tensor_copy)
+        quantise_w(3, nc.scalar.copy)
+        quantise_x(1, nc.scalar.copy)
+        project_queries(0)
+        project_queries(1)
+        square_and_sum(0)
+        square_and_sum(1)
+        quantise_x(2, nc.scalar.copy)
+        quantise_x(3, nc.scalar.copy)
+        normalise(0)
+        rotate_and_store(0)
+        quantise_w(4, nc.scalar.copy)
+        quantise_w(5, nc.scalar.copy)
+        project_queries(2)
+        project_queries(3)
+        k_raw = psum.tile([P, HEADS, HD], F32, tag="bank")
         for f in range(FRAMES):
-            q_raw = acc.tile([P, HEADS * HD], F32, name="q_raw%d" % f)
-            project(q_raw[:], f, 0, HEADS * HD)
-            q_res = norm_and_rope(q_raw[:])
-            nc.sync.dma_start(out=out_0[f].rearrange("s h c -> s (h c)"), in_=q_res[:].rearrange("p h c -> p (h c)"))
-
-        k_raw = acc.tile([P, FRAMES * P], F32)
-        v_raw = acc.tile([P, FRAMES * P], F32)
+            project(k_raw[:].rearrange("p h c -> p (h c)")[:, f * P : (f + 1) * P], f, 4 * P, P)
+        raws.append(k_raw)
+        v_raw = psum.tile([P, FRAMES, P], F32, tag="bank")
         for f in range(FRAMES):
-            project(k_raw[:, f * P : (f + 1) * P], f, 4 * P, P)
-        for f in range(FRAMES):
-            project(v_raw[:, f * P : (f + 1) * P], f, 5 * P, P)
+            project(v_raw[:, f, :], f, 5 * P, P)
+        for u in range(1, UNITS):
+            if u + 1 < UNITS:
+                square_and_sum(u + 1)
+            normalise(u)
+            rotate_and_store(u)
         v_res = keep.tile([P, FRAMES, P], F32)
-        nc.scalar.copy(out=v_res[:], in_=v_raw[:].rearrange("p (f c) -> p f c", c=P))
-        nc.sync.dma_start(out=out_2.rearrange("f s g c -> s f (g c)"), in_=v_res[:])
-        k_res = norm_and_rope(k_raw[:])
-        nc.sync.dma_start(
-            out=out_1.rearrange("f s g c -> s f (g c)"),
-            in_=k_res[:].rearrange("p (f g) c -> p f (g c)", f=FRAMES),
-        )
+        nc.scalar.copy(out=v_res[:], in_=v_raw[:])
+        nc.scalar.dma_start(out=out_2.rearrange("f s g c -> s f (g c)"), in_=v_res[:])

@@ -24,7 +24,7 @@ FREQS = 5
 ROT = 2 * FREQS
 UNITS = FRAMES + 1
 BANKS = 8
-POOL_UNITS = 4
+POOL_UNITS = 3
 W_TILES = 6
 ROPE_THETA = 10000.0
 QK_NORM_EPS = 1e-10
@@ -116,7 +116,7 @@ def tile_spatiotemporalattention_pa_s_kernel(tc, x, w_qkv, out_0, out_1, out_2):
         x_scales = keep.tile([P, FRAMES * P], U8, align_bytes=64)
         w_scales = keep.tile([P, W_TILES * P], U8, align_bytes=64)
 
-        def quantise_tile(rows_sb, t, grouped, codes, scales, copy):
+        def regroup_tile(rows_sb, t, grouped, copy):
             words = rows_sb[:, t, :].bitcast(F32)
             flipped = psum.tile([P, HALVES, P], F32, tag="bank")
             for u in range(HALVES):
@@ -127,17 +127,23 @@ def tile_spatiotemporalattention_pa_s_kernel(tc, x, w_qkv, out_0, out_1, out_2):
                 .rearrange("p (r u) -> p r u", u=HALVES),
                 in_=flipped[:].rearrange("p u r -> p r u"),
             )
+
+        def quantise(first, count, grouped, codes, scales):
             nc.vector.quantize_mx(
-                out=codes[:, t * P : (t + 1) * P].bitcast(FP8X4),
-                scales=scales[:, t * P : (t + 1) * P],
-                in_=grouped[:, t * D : (t + 1) * D],
+                out=codes[:, first * P : (first + count) * P].bitcast(FP8X4),
+                scales=scales[:, first * P : (first + count) * P],
+                in_=grouped[:, first * D : (first + count) * D],
             )
 
-        def quantise_x(f, copy):
-            quantise_tile(x_sb, f, x_grouped, x_codes, x_scales, copy)
+        def quantise_x(first, count, copy):
+            for f in range(first, first + count):
+                regroup_tile(x_sb, f, x_grouped, copy)
+            quantise(first, count, x_grouped, x_codes, x_scales)
 
-        def quantise_w(t, copy):
-            quantise_tile(w_sb, t, w_grouped, w_codes, w_scales, copy)
+        def quantise_w(first, count, copy):
+            for t in range(first, first + count):
+                regroup_tile(w_sb, t, w_grouped, copy)
+            quantise(first, count, w_grouped, w_codes, w_scales)
 
         def project(out, frame, first_col, cols):
             nc.tensor.matmul_mx(
@@ -204,24 +210,19 @@ def tile_spatiotemporalattention_pa_s_kernel(tc, x, w_qkv, out_0, out_1, out_2):
                     in_=res[:].rearrange("p (f g) c -> p f (g c)", f=FRAMES),
                 )
 
-        quantise_x(0, nc.vector.tensor_copy)
-        quantise_w(0, nc.vector.tensor_copy)
-        quantise_w(1, nc.scalar.copy)
-        quantise_w(2, nc.vector.tensor_copy)
-        quantise_w(3, nc.scalar.copy)
-        quantise_x(1, nc.scalar.copy)
-        project_queries(0)
-        project_queries(1)
-        square_and_sum(0)
-        square_and_sum(1)
-        quantise_x(2, nc.scalar.copy)
-        quantise_x(3, nc.scalar.copy)
-        normalise(0)
-        rotate_and_store(0)
-        quantise_w(4, nc.scalar.copy)
-        quantise_w(5, nc.scalar.copy)
-        project_queries(2)
-        project_queries(3)
+        quantise_x(0, 1, nc.vector.tensor_copy)
+        quantise_w(0, 1, nc.vector.tensor_copy)
+        quantise_w(1, 1, nc.scalar.copy)
+        quantise_w(2, 1, nc.vector.tensor_copy)
+        quantise_w(3, 1, nc.scalar.copy)
+        quantise_x(1, 1, nc.scalar.copy)
+        quantise_x(2, 1, nc.scalar.copy)
+        quantise_x(3, 1, nc.scalar.copy)
+        quantise_w(4, 1, nc.scalar.copy)
+        quantise_w(5, 1, nc.scalar.copy)
+
+        for f in range(FRAMES):
+            project_queries(f)
         k_raw = psum.tile([P, HEADS, HD], F32, tag="bank")
         for f in range(FRAMES):
             project(k_raw[:].rearrange("p h c -> p (h c)")[:, f * P : (f + 1) * P], f, 4 * P, P)
@@ -229,7 +230,9 @@ def tile_spatiotemporalattention_pa_s_kernel(tc, x, w_qkv, out_0, out_1, out_2):
         v_raw = psum.tile([P, FRAMES, P], F32, tag="bank")
         for f in range(FRAMES):
             project(v_raw[:, f, :], f, 5 * P, P)
-        for u in range(1, UNITS):
+
+        square_and_sum(0)
+        for u in range(UNITS):
             if u + 1 < UNITS:
                 square_and_sum(u + 1)
             normalise(u)

@@ -19,13 +19,18 @@ D = 512
 HALVES = 2
 HD = 32
 HEADS = 16
+GROUPS = 4
 GRID_W = 16
 FREQS = 5
 ROT = 2 * FREQS
-UNITS = FRAMES + 1
-BANKS = 8
-POOL_UNITS = 3
 W_TILES = 6
+KEY_TILE = 4
+VALUE_TILE = 5
+BANKS = 8
+UNITS = FRAMES + 1
+KEY_UNIT = 3
+POOL_UNITS = 3
+VECTOR_COPIES = 3
 ROPE_THETA = 10000.0
 QK_NORM_EPS = 1e-10
 ROUND_MAGIC = 12582912.0
@@ -44,7 +49,7 @@ def tile_spatiotemporalattention_pa_s_kernel(tc, x, w_qkv, out_0, out_1, out_2):
         x_sb = keep.tile([P, FRAMES, D], BF16)
         w_sb = keep.tile([P, W_TILES, D], BF16)
         nc.sync.dma_start(out=x_sb[:, 0, :], in_=x_tiles[:, 0, :])
-        for t in range(4):
+        for t in range(KEY_TILE):
             nc.sync.dma_start(out=w_sb[:, t, :], in_=w_tiles[:, t, :])
         nc.sync.dma_start(out=x_sb[:, 1, :], in_=x_tiles[:, 1, :])
         nc.sync.dma_start(out=x_sb[:, 2:4, :], in_=x_tiles[:, 2:4, :])
@@ -102,22 +107,29 @@ def tile_spatiotemporalattention_pa_s_kernel(tc, x, w_qkv, out_0, out_1, out_2):
         nc.scalar.activation(
             out=table[:, 0, :], in_=part[:, 1, :], func=FUNC.Sin, scale=-2.0 * math.pi
         )
+        cos_sin = table[:, 1:3, :].unsqueeze(1).to_broadcast([P, HEADS, 2, FREQS])
+        nsin_cos = table[:, 0:2, :].unsqueeze(1).to_broadcast([P, HEADS, 2, FREQS])
         one = keep.tile([P, 1], F32)
         nc.vector.memset(one[:], 1.0)
         warm_rsqrt = keep.tile([P, 1], F32)
         nc.scalar.activation(out=warm_rsqrt[:], in_=one[:], func=FUNC.Abs_reciprocal_sqrt)
-        cos_sin = table[:, 1:3, :].unsqueeze(1).to_broadcast([P, HEADS, 2, FREQS])
-        nsin_cos = table[:, 0:2, :].unsqueeze(1).to_broadcast([P, HEADS, 2, FREQS])
 
-        x_grouped = keep.tile([P, FRAMES * D], BF16, align_bytes=64)
-        w_grouped = keep.tile([P, W_TILES * D], BF16, align_bytes=64)
-        x_codes = keep.tile([P, FRAMES * P], U32, align_bytes=64)
-        w_codes = keep.tile([P, W_TILES * P], U32, align_bytes=64)
-        x_scales = keep.tile([P, FRAMES * P], U8, align_bytes=64)
-        w_scales = keep.tile([P, W_TILES * P], U8, align_bytes=64)
+        x_op = (
+            x_sb,
+            keep.tile([P, FRAMES * D], BF16, align_bytes=64, name="x_grouped"),
+            keep.tile([P, FRAMES * P], U32, align_bytes=64, name="x_codes"),
+            keep.tile([P, FRAMES * P], U8, align_bytes=64, name="x_scales"),
+        )
+        w_op = (
+            w_sb,
+            keep.tile([P, W_TILES * D], BF16, align_bytes=64, name="w_grouped"),
+            keep.tile([P, W_TILES * P], U32, align_bytes=64, name="w_codes"),
+            keep.tile([P, W_TILES * P], U8, align_bytes=64, name="w_scales"),
+        )
 
-        def regroup_tile(rows_sb, t, grouped, copy):
-            words = rows_sb[:, t, :].bitcast(F32)
+        def quantise_tile(operand, t, copy):
+            rows, grouped, codes, scales = operand
+            words = rows[:, t, :].bitcast(F32)
             flipped = psum.tile([P, HALVES, P], F32, tag="bank")
             for u in range(HALVES):
                 nc.tensor.transpose(flipped[:, u, :], words[:, u * P : (u + 1) * P], ident[:])
@@ -127,43 +139,51 @@ def tile_spatiotemporalattention_pa_s_kernel(tc, x, w_qkv, out_0, out_1, out_2):
                 .rearrange("p (r u) -> p r u", u=HALVES),
                 in_=flipped[:].rearrange("p u r -> p r u"),
             )
-
-        def quantise(first, count, grouped, codes, scales):
             nc.vector.quantize_mx(
-                out=codes[:, first * P : (first + count) * P].bitcast(FP8X4),
-                scales=scales[:, first * P : (first + count) * P],
-                in_=grouped[:, first * D : (first + count) * D],
+                out=codes[:, t * P : (t + 1) * P].bitcast(FP8X4),
+                scales=scales[:, t * P : (t + 1) * P],
+                in_=grouped[:, t * D : (t + 1) * D],
             )
 
-        def quantise_x(first, count, copy):
-            for f in range(first, first + count):
-                regroup_tile(x_sb, f, x_grouped, copy)
-            quantise(first, count, x_grouped, x_codes, x_scales)
+        in_load_order = (
+            [(x_op, 0)]
+            + [(w_op, t) for t in range(KEY_TILE)]
+            + [(x_op, f) for f in range(1, FRAMES)]
+            + [(w_op, KEY_TILE), (w_op, VALUE_TILE)]
+        )
+        for n, (operand, t) in enumerate(in_load_order):
+            quantise_tile(
+                operand, t, nc.vector.tensor_copy if n < VECTOR_COPIES else nc.scalar.copy
+            )
 
-        def quantise_w(first, count, copy):
-            for t in range(first, first + count):
-                regroup_tile(w_sb, t, w_grouped, copy)
-            quantise(first, count, w_grouped, w_codes, w_scales)
-
-        def project(out, frame, first_col, cols):
+        def project(out, frame, first_tile, tiles):
+            cols = slice(first_tile * P, (first_tile + tiles) * P)
             nc.tensor.matmul_mx(
                 out=out,
-                lhsT=x_codes[:, frame * P : (frame + 1) * P].bitcast(FP8X4),
-                lhsT_scale=x_scales[:, frame * P : (frame + 1) * P],
-                rhs=w_codes[:, first_col : first_col + cols].bitcast(FP8X4),
-                rhs_scale=w_scales[:, first_col : first_col + cols],
+                lhsT=x_op[2][:, frame * P : (frame + 1) * P].bitcast(FP8X4),
+                lhsT_scale=x_op[3][:, frame * P : (frame + 1) * P],
+                rhs=w_op[2][:, cols].bitcast(FP8X4),
+                rhs_scale=w_op[3][:, cols],
                 start=True,
                 stop=True,
             )
 
-        raws = []
+        q_raws = []
+        for f in range(FRAMES):
+            q_raw = psum.tile([P, HEADS, HD], F32, tag="bank")
+            project(q_raw[:].rearrange("p h c -> p (h c)"), f, 0, KEY_TILE)
+            q_raws.append(q_raw)
+        k_raw = psum.tile([P, FRAMES, GROUPS * HD], F32, tag="bank")
+        v_raw = psum.tile([P, FRAMES, GROUPS * HD], F32, tag="bank")
+        for f in range(FRAMES):
+            project(k_raw[:, f, :], f, KEY_TILE, 1)
+        for f in range(FRAMES):
+            project(v_raw[:, f, :], f, VALUE_TILE, 1)
+        keys = k_raw[:].rearrange("p f (g c) -> p (f g) c", c=HD)
+        raws = q_raws[:KEY_UNIT] + [keys] + q_raws[KEY_UNIT:]
+
         sumsqs = []
         results = []
-
-        def project_queries(f):
-            q_raw = psum.tile([P, HEADS, HD], F32, tag="bank")
-            project(q_raw[:].rearrange("p h c -> p (h c)"), f, 0, HEADS * HD)
-            raws.append(q_raw)
 
         def square_and_sum(u):
             squares = unit.tile([P, HEADS, HD], F32)
@@ -186,57 +206,51 @@ def tile_spatiotemporalattention_pa_s_kernel(tc, x, w_qkv, out_0, out_1, out_2):
             )
             results.append(res)
 
-        def rotate_and_store(u):
-            engine = nc.gpsimd if u < POOL_UNITS else nc.vector
-            res = results[u]
-            pairs = res[:, :, 0:ROT].rearrange("p h (m e) -> p h m e", e=2)
-            even = pairs[:, :, :, 0].unsqueeze(2).to_broadcast([P, HEADS, 2, FREQS])
-            odd = pairs[:, :, :, 1].unsqueeze(2).to_broadcast([P, HEADS, 2, FREQS])
-            from_even = unit.tile([P, HEADS, 2, FREQS], F32)
-            from_odd = unit.tile([P, HEADS, 2, FREQS], F32)
-            engine.tensor_tensor(out=from_even[:], in0=even, in1=cos_sin, op=ALU.mult)
-            engine.tensor_tensor(out=from_odd[:], in0=odd, in1=nsin_cos, op=ALU.mult)
-            engine.tensor_tensor(
-                out=res[:, :, 0:ROT].rearrange("p h (o m) -> p h o m", o=2),
-                in0=from_even[:],
-                in1=from_odd[:],
-                op=ALU.add,
-            )
-            if u < FRAMES:
-                nc.sync.dma_start(out=out_0[u], in_=res[:])
-            else:
-                nc.sync.dma_start(
-                    out=out_1.rearrange("f s g c -> s f (g c)"),
-                    in_=res[:].rearrange("p (f g) c -> p f (g c)", f=FRAMES),
+        def rotate_and_store(units, engine):
+            from_even = {}
+            from_odd = {}
+            for u in units:
+                pairs = results[u][:, :, 0:ROT].rearrange("p h (m e) -> p h m e", e=2)
+                from_even[u] = unit.tile([P, HEADS, 2, FREQS], F32, name="from_even")
+                engine.tensor_tensor(
+                    out=from_even[u][:],
+                    in0=pairs[:, :, :, 0].unsqueeze(2).to_broadcast([P, HEADS, 2, FREQS]),
+                    in1=cos_sin,
+                    op=ALU.mult,
                 )
-
-        quantise_x(0, 1, nc.vector.tensor_copy)
-        quantise_w(0, 1, nc.vector.tensor_copy)
-        quantise_w(1, 1, nc.scalar.copy)
-        quantise_w(2, 1, nc.vector.tensor_copy)
-        quantise_w(3, 1, nc.scalar.copy)
-        quantise_x(1, 1, nc.scalar.copy)
-        quantise_x(2, 1, nc.scalar.copy)
-        quantise_x(3, 1, nc.scalar.copy)
-        quantise_w(4, 1, nc.scalar.copy)
-        quantise_w(5, 1, nc.scalar.copy)
-
-        for f in range(FRAMES):
-            project_queries(f)
-        k_raw = psum.tile([P, HEADS, HD], F32, tag="bank")
-        for f in range(FRAMES):
-            project(k_raw[:].rearrange("p h c -> p (h c)")[:, f * P : (f + 1) * P], f, 4 * P, P)
-        raws.append(k_raw)
-        v_raw = psum.tile([P, FRAMES, P], F32, tag="bank")
-        for f in range(FRAMES):
-            project(v_raw[:, f, :], f, 5 * P, P)
+            for u in units:
+                pairs = results[u][:, :, 0:ROT].rearrange("p h (m e) -> p h m e", e=2)
+                from_odd[u] = unit.tile([P, HEADS, 2, FREQS], F32, name="from_odd")
+                engine.tensor_tensor(
+                    out=from_odd[u][:],
+                    in0=pairs[:, :, :, 1].unsqueeze(2).to_broadcast([P, HEADS, 2, FREQS]),
+                    in1=nsin_cos,
+                    op=ALU.mult,
+                )
+            for u in units:
+                engine.tensor_tensor(
+                    out=results[u][:, :, 0:ROT].rearrange("p h (o m) -> p h o m", o=2),
+                    in0=from_even[u][:],
+                    in1=from_odd[u][:],
+                    op=ALU.add,
+                )
+                if u == KEY_UNIT:
+                    nc.sync.dma_start(
+                        out=out_1.rearrange("f s g c -> s f (g c)"),
+                        in_=results[u][:].rearrange("p (f g) c -> p f (g c)", f=FRAMES),
+                    )
+                else:
+                    nc.sync.dma_start(out=out_0[u if u < KEY_UNIT else u - 1], in_=results[u][:])
 
         square_and_sum(0)
         for u in range(UNITS):
             if u + 1 < UNITS:
                 square_and_sum(u + 1)
             normalise(u)
-            rotate_and_store(u)
-        v_res = keep.tile([P, FRAMES, P], F32)
+            if u < POOL_UNITS:
+                rotate_and_store([u], nc.gpsimd)
+        rotate_and_store(list(range(POOL_UNITS, UNITS)), nc.vector)
+
+        v_res = keep.tile([P, FRAMES, GROUPS * HD], F32)
         nc.scalar.copy(out=v_res[:], in_=v_raw[:])
         nc.scalar.dma_start(out=out_2.rearrange("f s g c -> s f (g c)"), in_=v_res[:])

@@ -28,7 +28,6 @@ KEY_TILE = 4
 VALUE_TILE = 5
 BANKS = 8
 UNITS = FRAMES + 1
-KEY_UNIT = 3
 POOL_UNITS = 3
 VECTOR_COPIES = 3
 ROPE_THETA = 10000.0
@@ -179,8 +178,7 @@ def tile_spatiotemporalattention_pa_s_kernel(tc, x, w_qkv, out_0, out_1, out_2):
             project(k_raw[:, f, :], f, KEY_TILE, 1)
         for f in range(FRAMES):
             project(v_raw[:, f, :], f, VALUE_TILE, 1)
-        keys = k_raw[:].rearrange("p f (g c) -> p (f g) c", c=HD)
-        raws = q_raws[:KEY_UNIT] + [keys] + q_raws[KEY_UNIT:]
+        raws = q_raws + [k_raw[:].rearrange("p f (g c) -> p (f g) c", c=HD)]
 
         sumsqs = []
         results = []
@@ -206,7 +204,7 @@ def tile_spatiotemporalattention_pa_s_kernel(tc, x, w_qkv, out_0, out_1, out_2):
             )
             results.append(res)
 
-        def rotate_and_store(units, engine):
+        def rotate_and_store(units, engine, queue):
             from_even = {}
             from_odd = {}
             for u in units:
@@ -234,23 +232,26 @@ def tile_spatiotemporalattention_pa_s_kernel(tc, x, w_qkv, out_0, out_1, out_2):
                     in1=from_odd[u][:],
                     op=ALU.add,
                 )
-                if u == KEY_UNIT:
-                    nc.sync.dma_start(
+                if u < FRAMES:
+                    queue.dma_start(out=out_0[u], in_=results[u][:])
+                else:
+                    queue.dma_start(
                         out=out_1.rearrange("f s g c -> s f (g c)"),
                         in_=results[u][:].rearrange("p (f g) c -> p f (g c)", f=FRAMES),
                     )
-                else:
-                    nc.sync.dma_start(out=out_0[u if u < KEY_UNIT else u - 1], in_=results[u][:])
+
+        def copy_values():
+            v_res = keep.tile([P, FRAMES, GROUPS * HD], F32)
+            nc.scalar.copy(out=v_res[:], in_=v_raw[:])
+            nc.scalar.dma_start(out=out_2.rearrange("f s g c -> s f (g c)"), in_=v_res[:])
 
         square_and_sum(0)
         for u in range(UNITS):
             if u + 1 < UNITS:
                 square_and_sum(u + 1)
+            if u + 1 == UNITS - 1:
+                copy_values()
             normalise(u)
             if u < POOL_UNITS:
-                rotate_and_store([u], nc.gpsimd)
-        rotate_and_store(list(range(POOL_UNITS, UNITS)), nc.vector)
-
-        v_res = keep.tile([P, FRAMES, GROUPS * HD], F32)
-        nc.scalar.copy(out=v_res[:], in_=v_raw[:])
-        nc.scalar.dma_start(out=out_2.rearrange("f s g c -> s f (g c)"), in_=v_res[:])
+                rotate_and_store([u], nc.gpsimd, nc.sync)
+        rotate_and_store(list(range(POOL_UNITS, UNITS)), nc.vector, nc.scalar)

@@ -50,9 +50,10 @@ def tile_spatiotemporalattention_pa_s_kernel(tc, x, w_qkv, out_0, out_1, out_2):
         nc.sync.dma_start(out=x_sb[:, 0, :], in_=x_tiles[:, 0, :])
         for t in range(KEY_TILE):
             nc.sync.dma_start(out=w_sb[:, t, :], in_=w_tiles[:, t, :])
-        nc.sync.dma_start(out=x_sb[:, 1, :], in_=x_tiles[:, 1, :])
-        nc.sync.dma_start(out=x_sb[:, 2:4, :], in_=x_tiles[:, 2:4, :])
-        nc.sync.dma_start(out=w_sb[:, 4:6, :], in_=w_tiles[:, 4:6, :])
+        for f in range(1, FRAMES):
+            nc.sync.dma_start(out=x_sb[:, f, :], in_=x_tiles[:, f, :])
+        for t in (KEY_TILE, VALUE_TILE):
+            nc.sync.dma_start(out=w_sb[:, t, :], in_=w_tiles[:, t, :])
 
         zero = keep.tile([P, 1], F32)
         nc.vector.memset(zero[:], 0.0)

@@ -28,6 +28,7 @@ KEY_TILE = 4
 VALUE_TILE = 5
 BANKS = 8
 UNITS = FRAMES + 1
+KEY_UNIT = 3
 POOL_UNITS = 3
 VECTOR_COPIES = 3
 ROPE_THETA = 10000.0
@@ -179,7 +180,8 @@ def tile_spatiotemporalattention_pa_s_kernel(tc, x, w_qkv, out_0, out_1, out_2):
             project(k_raw[:, f, :], f, KEY_TILE, 1)
         for f in range(FRAMES):
             project(v_raw[:, f, :], f, VALUE_TILE, 1)
-        raws = q_raws + [k_raw[:].rearrange("p f (g c) -> p (f g) c", c=HD)]
+        keys = k_raw[:].rearrange("p f (g c) -> p (f g) c", c=HD)
+        raws = q_raws[:KEY_UNIT] + [keys] + q_raws[KEY_UNIT:]
 
         sumsqs = []
         results = []
@@ -205,41 +207,40 @@ def tile_spatiotemporalattention_pa_s_kernel(tc, x, w_qkv, out_0, out_1, out_2):
             )
             results.append(res)
 
-        def rotate_and_store(units, engine, queue):
-            from_even = {}
-            from_odd = {}
-            for u in units:
-                pairs = results[u][:, :, 0:ROT].rearrange("p h (m e) -> p h m e", e=2)
-                from_even[u] = unit.tile([P, HEADS, 2, FREQS], F32, name="from_even")
-                engine.tensor_tensor(
-                    out=from_even[u][:],
-                    in0=pairs[:, :, :, 0].unsqueeze(2).to_broadcast([P, HEADS, 2, FREQS]),
-                    in1=cos_sin,
-                    op=ALU.mult,
+        def rotate(u):
+            engine = nc.gpsimd if u < POOL_UNITS else nc.vector
+            res = results[u]
+            pairs = res[:, :, 0:ROT].rearrange("p h (m e) -> p h m e", e=2)
+            from_even = unit.tile([P, HEADS, 2, FREQS], F32)
+            from_odd = unit.tile([P, HEADS, 2, FREQS], F32)
+            engine.tensor_tensor(
+                out=from_even[:],
+                in0=pairs[:, :, :, 0].unsqueeze(2).to_broadcast([P, HEADS, 2, FREQS]),
+                in1=cos_sin,
+                op=ALU.mult,
+            )
+            engine.tensor_tensor(
+                out=from_odd[:],
+                in0=pairs[:, :, :, 1].unsqueeze(2).to_broadcast([P, HEADS, 2, FREQS]),
+                in1=nsin_cos,
+                op=ALU.mult,
+            )
+            engine.tensor_tensor(
+                out=res[:, :, 0:ROT].rearrange("p h (o m) -> p h o m", o=2),
+                in0=from_even[:],
+                in1=from_odd[:],
+                op=ALU.add,
+            )
+
+        def store(u):
+            queue = nc.sync if u < POOL_UNITS else nc.scalar
+            if u == KEY_UNIT:
+                queue.dma_start(
+                    out=out_1.rearrange("f s g c -> s f (g c)"),
+                    in_=results[u][:].rearrange("p (f g) c -> p f (g c)", f=FRAMES),
                 )
-            for u in units:
-                pairs = results[u][:, :, 0:ROT].rearrange("p h (m e) -> p h m e", e=2)
-                from_odd[u] = unit.tile([P, HEADS, 2, FREQS], F32, name="from_odd")
-                engine.tensor_tensor(
-                    out=from_odd[u][:],
-                    in0=pairs[:, :, :, 1].unsqueeze(2).to_broadcast([P, HEADS, 2, FREQS]),
-                    in1=nsin_cos,
-                    op=ALU.mult,
-                )
-            for u in units:
-                engine.tensor_tensor(
-                    out=results[u][:, :, 0:ROT].rearrange("p h (o m) -> p h o m", o=2),
-                    in0=from_even[u][:],
-                    in1=from_odd[u][:],
-                    op=ALU.add,
-                )
-                if u < FRAMES:
-                    queue.dma_start(out=out_0[u], in_=results[u][:])
-                else:
-                    queue.dma_start(
-                        out=out_1.rearrange("f s g c -> s f (g c)"),
-                        in_=results[u][:].rearrange("p (f g) c -> p f (g c)", f=FRAMES),
-                    )
+            else:
+                queue.dma_start(out=out_0[u if u < KEY_UNIT else u - 1], in_=results[u][:])
 
         def copy_values():
             v_res = keep.tile([P, FRAMES, GROUPS * HD], F32)
@@ -253,6 +254,7 @@ def tile_spatiotemporalattention_pa_s_kernel(tc, x, w_qkv, out_0, out_1, out_2):
             if u + 1 == UNITS - 1:
                 copy_values()
             normalise(u)
-            if u < POOL_UNITS:
-                rotate_and_store([u], nc.gpsimd, nc.sync)
-        rotate_and_store(list(range(POOL_UNITS, UNITS)), nc.vector, nc.scalar)
+            if u > 0:
+                store(u - 1)
+            rotate(u)
+        store(UNITS - 1)

import math

import concourse.mybir as mybir
from concourse.masks import make_identity

F32 = mybir.dt.float32
BF16 = mybir.dt.bfloat16
I32 = mybir.dt.int32
U32 = mybir.dt.uint32
U8 = mybir.dt.uint8
FP8X4 = mybir.dt.float8_e4m3fn_x4
ALU = mybir.AluOpType
FUNC = mybir.ActivationFunctionType
AXIS = mybir.AxisListType

P = 128
FRAMES = 4
D = 512
HALVES = 2
HD = 32
HEADS = 16
GROUPS = 4
GRID_W = 16
FREQS = 5
ROT = 2 * FREQS
W_TILES = 6
KEY_TILE = 4
VALUE_TILE = 5
BANKS = 8
UNITS = FRAMES + 1
KEY_UNIT = 3
POOL_UNITS = 3
VECTOR_COPIES = 3
ROPE_THETA = 10000.0
QK_NORM_EPS = 1e-10
ROUND_MAGIC = 12582912.0

FLOPS = 2 * FRAMES * P * D * W_TILES * P


def tile_spatiotemporalattention_pa_s_kernel(tc, x, w_qkv, out_0, out_1, out_2):
    nc = tc.nc
    x_tiles = x.rearrange("b t s d -> s (b t) d")
    w_tiles = w_qkv.rearrange("(t r) d -> r t d", r=P)

    with tc.tile_pool(name="keep", bufs=1) as keep, tc.tile_pool(
        name="unit", bufs=UNITS
    ) as unit, tc.psum_pool(name="psum", bufs=BANKS) as psum, tc.manual_schedule():
        x_sb = keep.tile([P, FRAMES, D], BF16)
        w_sb = keep.tile([P, W_TILES, D], BF16)
        nc.sync.dma_start(out=x_sb[:, 0, :], in_=x_tiles[:, 0, :])
        for t in range(KEY_TILE):
            nc.sync.dma_start(out=w_sb[:, t, :], in_=w_tiles[:, t, :])
        for f in range(1, FRAMES):
            nc.sync.dma_start(out=x_sb[:, f, :], in_=x_tiles[:, f, :])
        for t in (KEY_TILE, VALUE_TILE):
            nc.sync.dma_start(out=w_sb[:, t, :], in_=w_tiles[:, t, :])

        zero = keep.tile([P, 1], F32)
        nc.vector.memset(zero[:], 0.0)
        warm_sin = keep.tile([P, 1], F32)
        nc.scalar.activation(out=warm_sin[:], in_=zero[:], func=FUNC.Sin)

        patch = keep.tile([P, 1], I32)
        nc.gpsimd.iota(patch[:], pattern=[[0, 1]], base=0, channel_multiplier=1)
        ident = keep.tile([P, P], F32)
        make_identity(nc, ident[:])

        grid_row = keep.tile([P, 1], I32)
        nc.vector.tensor_single_scalar(
            out=grid_row[:], in_=patch[:], scalar=4, op=ALU.arith_shift_right
        )
        steps = keep.tile([P, 1], F32)
        nc.vector.scalar_tensor_tensor(
            out=steps[:],
            in0=grid_row[:],
            scalar=float(1 - GRID_W),
            in1=patch[:],
            op0=ALU.mult,
            op1=ALU.add,
        )
        quarter = keep.tile([P, 2], F32)
        nc.vector.memset(quarter[:, 0:1], 0.25)
        nc.vector.memset(quarter[:, 1:2], 0.0)
        turns = keep.tile([P, 2, FREQS], F32)
        for m in range(FREQS):
            nc.vector.scalar_tensor_tensor(
                out=turns[:, :, m],
                in0=steps[:, 0:1].to_broadcast([P, 2]),
                scalar=ROPE_THETA ** (-2.0 * m / ROT) / (2.0 * math.pi),
                in1=quarter[:],
                op0=ALU.mult,
                op1=ALU.add,
            )
        whole = keep.tile([P, 2, FREQS], F32)
        nc.vector.tensor_scalar(
            out=whole[:],
            in0=turns[:],
            scalar1=ROUND_MAGIC,
            scalar2=ROUND_MAGIC,
            op0=ALU.add,
            op1=ALU.subtract,
        )
        part = keep.tile([P, 2, FREQS], F32)
        nc.vector.tensor_tensor(out=part[:], in0=turns[:], in1=whole[:], op=ALU.subtract)
        table = keep.tile([P, 3, FREQS], F32)
        nc.scalar.activation(out=table[:, 1:3, :], in_=part[:], func=FUNC.Sin, scale=2.0 * math.pi)
        nc.scalar.activation(
            out=table[:, 0, :], in_=part[:, 1, :], func=FUNC.Sin, scale=-2.0 * math.pi
        )
        cos_sin = table[:, 1:3, :].unsqueeze(1).to_broadcast([P, HEADS, 2, FREQS])
        nsin_cos = table[:, 0:2, :].unsqueeze(1).to_broadcast([P, HEADS, 2, FREQS])
        one = keep.tile([P, 1], F32)
        nc.vector.memset(one[:], 1.0)
        warm_rsqrt = keep.tile([P, 1], F32)
        nc.scalar.activation(out=warm_rsqrt[:], in_=one[:], func=FUNC.Abs_reciprocal_sqrt)

        x_op = (
            x_sb,
            keep.tile([P, FRAMES * D], BF16, align_bytes=64, name="x_grouped"),
            keep.tile([P, FRAMES * P], U32, align_bytes=64, name="x_codes"),
            keep.tile([P, FRAMES * P], U8, align_bytes=64, name="x_scales"),
        )
        w_op = (
            w_sb,
            keep.tile([P, W_TILES * D], BF16, align_bytes=64, name="w_grouped"),
            keep.tile([P, W_TILES * P], U32, align_bytes=64, name="w_codes"),
            keep.tile([P, W_TILES * P], U8, align_bytes=64, name="w_scales"),
        )

        def quantise_tile(operand, t, copy):
            rows, grouped, codes, scales = operand
            words = rows[:, t, :].bitcast(F32)
            flipped = psum.tile([P, HALVES, P], F32, tag="bank")
            for u in range(HALVES):
                nc.tensor.transpose(flipped[:, u, :], words[:, u * P : (u + 1) * P], ident[:])
            copy(
                out=grouped[:, t * D : (t + 1) * D]
                .bitcast(F32)
                .rearrange("p (r u) -> p r u", u=HALVES),
                in_=flipped[:].rearrange("p u r -> p r u"),
            )
            nc.vector.quantize_mx(
                out=codes[:, t * P : (t + 1) * P].bitcast(FP8X4),
                scales=scales[:, t * P : (t + 1) * P],
                in_=grouped[:, t * D : (t + 1) * D],
            )

        in_load_order = (
            [(x_op, 0)]
            + [(w_op, t) for t in range(KEY_TILE)]
            + [(x_op, f) for f in range(1, FRAMES)]
            + [(w_op, KEY_TILE), (w_op, VALUE_TILE)]
        )
        for n, (operand, t) in enumerate(in_load_order):
            quantise_tile(
                operand, t, nc.vector.tensor_copy if n < VECTOR_COPIES else nc.scalar.copy
            )

        def project(out, frame, first_tile, tiles):
            cols = slice(first_tile * P, (first_tile + tiles) * P)
            nc.tensor.matmul_mx(
                out=out,
                lhsT=x_op[2][:, frame * P : (frame + 1) * P].bitcast(FP8X4),
                lhsT_scale=x_op[3][:, frame * P : (frame + 1) * P],
                rhs=w_op[2][:, cols].bitcast(FP8X4),
                rhs_scale=w_op[3][:, cols],
                start=True,
                stop=True,
            )

        q_raws = []
        for f in range(FRAMES):
            q_raw = psum.tile([P, HEADS, HD], F32, tag="bank")
            project(q_raw[:].rearrange("p h c -> p (h c)"), f, 0, KEY_TILE)
            q_raws.append(q_raw)
        k_raw = psum.tile([P, FRAMES, GROUPS * HD], F32, tag="bank")
        v_raw = psum.tile([P, FRAMES, GROUPS * HD], F32, tag="bank")
        for f in range(FRAMES):
            project(k_raw[:, f, :], f, KEY_TILE, 1)
        for f in range(FRAMES):
            project(v_raw[:, f, :], f, VALUE_TILE, 1)
        keys = k_raw[:].rearrange("p f (g c) -> p (f g) c", c=HD)
        raws = q_raws[:KEY_UNIT] + [keys] + q_raws[KEY_UNIT:]

        sumsqs = []
        results = []

        def square_and_sum(u):
            squares = unit.tile([P, HEADS, HD], F32)
            nc.scalar.activation(out=squares[:], in_=raws[u][:], func=FUNC.Square)
            sumsq = unit.tile([P, HEADS], F32)
            nc.vector.tensor_reduce(out=sumsq[:], in_=squares[:], axis=AXIS.X, op=ALU.add)
            sumsqs.append(sumsq)

        def normalise(u):
            inv = unit.tile([P, HEADS], F32)
            nc.scalar.activation(out=inv[:], in_=sumsqs[u][:], func=FUNC.Abs_reciprocal_sqrt)
            res = unit.tile([P, HEADS, HD], F32)
            nc.vector.scalar_tensor_tensor(
                out=res[:],
                in0=inv[:].unsqueeze(2).to_broadcast([P, HEADS, HD]),
                scalar=1.0 / QK_NORM_EPS,
                in1=raws[u][:],
                op0=ALU.min,
                op1=ALU.mult,
            )
            results.append(res)

        def rotate(u):
            engine = nc.gpsimd if u < POOL_UNITS else nc.vector
            res = results[u]
            pairs = res[:, :, 0:ROT].rearrange("p h (m e) -> p h m e", e=2)
            from_even = unit.tile([P, HEADS, 2, FREQS], F32)
            from_odd = unit.tile([P, HEADS, 2, FREQS], F32)
            engine.tensor_tensor(
                out=from_even[:],
                in0=pairs[:, :, :, 0].unsqueeze(2).to_broadcast([P, HEADS, 2, FREQS]),
                in1=cos_sin,
                op=ALU.mult,
            )
            engine.tensor_tensor(
                out=from_odd[:],
                in0=pairs[:, :, :, 1].unsqueeze(2).to_broadcast([P, HEADS, 2, FREQS]),
                in1=nsin_cos,
                op=ALU.mult,
            )
            engine.tensor_tensor(
                out=res[:, :, 0:ROT].rearrange("p h (o m) -> p h o m", o=2),
                in0=from_even[:],
                in1=from_odd[:],
                op=ALU.add,
            )

        def store(u):
            queue = nc.sync if u < POOL_UNITS else nc.scalar
            if u == KEY_UNIT:
                queue.dma_start(
                    out=out_1.rearrange("f s g c -> s f (g c)"),
                    in_=results[u][:].rearrange("p (f g) c -> p f (g c)", f=FRAMES),
                )
            else:
                queue.dma_start(out=out_0[u if u < KEY_UNIT else u - 1], in_=results[u][:])

        def copy_values():
            v_res = keep.tile([P, FRAMES, GROUPS * HD], F32)
            nc.scalar.copy(out=v_res[:], in_=v_raw[:])
            nc.scalar.dma_start(out=out_2.rearrange("f s g c -> s f (g c)"), in_=v_res[:])

        square_and_sum(0)
        for u in range(UNITS):
            if u + 1 < UNITS:
                square_and_sum(u + 1)
            if u + 1 == UNITS - 1:
                copy_values()
            normalise(u)
            if u > 0:
                store(u - 1)
            rotate(u)
        store(UNITS - 1)
